import numpy as np
import ml_dtypes

BF16 = ml_dtypes.bfloat16


def bf(x):
    return np.asarray(x, np.float32).astype(BF16)


def f32(x):
    return np.asarray(x, np.float32)


def f64(x):
    return np.asarray(x).astype(np.float64)


def striped(idx):
    return np.tile(idx.reshape(-1, 16).T, (8, 1))


E, H, D, T, L, S, N = 1024, 16, 64, 64, 128, 2048, 1024
SCALE = D ** -0.5
EPS = 1e-5


def ln(u, gain, shift):
    m = u.mean(axis=-1, keepdims=True)
    var = ((u - m) ** 2).mean(axis=-1, keepdims=True)
    return (u - m) / np.sqrt(var + EPS) * f64(gain)[:, 0] + f64(shift)[:, 0]


def setup_inputs():
    rn = np.random.standard_normal
    return {
        "reg_x": bf(rn((E, N))),
        "sum_x": bf(1.5 * rn((E, T))),
        "rel_emb": f32(rn((L, S))),
        "Wr0": bf(rn((L, E)) / np.sqrt(L)),
        "Wk": bf(rn((E, E)) / np.sqrt(E)),
        "bk": f32(0.1 * rn((E, 1))),
        "Wv": bf(rn((E, E)) / np.sqrt(E)),
        "bv": f32(0.1 * rn((E, 1))),
        "gain_k": f32(1.0 + 0.1 * rn((D, 1))),
        "shift_k": f32(0.1 * rn((D, 1))),
        "gain_v": f32(1.0 + 0.1 * rn((D, 1))),
        "shift_v": f32(0.1 * rn((D, 1))),
        "Wk2": bf(rn((D, D)) / np.sqrt(D)),
        "bk2": f32(0.1 * rn((D, 1))),
        "Wv2": bf(rn((D, D)) / np.sqrt(D)),
        "bv2": f32(0.1 * rn((D, 1))),
        "gain_k2": f32(1.0 + 0.1 * rn((D, 1))),
        "shift_k2": f32(0.1 * rn((D, 1))),
        "gain_v2": f32(1.0 + 0.1 * rn((D, 1))),
        "shift_v2": f32(0.1 * rn((D, 1))),
        "offs": striped(np.random.permutation(np.tile(np.arange(S), 2))[:N]),
    }


def reference(reg_x, sum_x, rel_emb, Wr0, Wk, bk, Wv, bv, gain_k, shift_k, gain_v, shift_v, Wk2, bk2, Wv2, bv2, gain_k2, shift_k2, gain_v2, shift_v2, offs):
    idx = offs[:16].T.reshape(-1)
    x = f64(reg_x).T
    k = ln((x @ f64(Wk) + f64(bk)[:, 0]).reshape(N, H, D), gain_k, shift_k)
    v = ln((x @ f64(Wv) + f64(bv)[:, 0]).reshape(N, H, D), gain_v, shift_v)
    r0 = (f64(Wr0).T @ f64(rel_emb)).reshape(H, D, S)
    q = f64(sum_x).reshape(H, D, T) * SCALE
    content = np.einsum('hdt,nhd->htn', q, k)
    qr = np.einsum('hdt,hdz->htz', q, r0)
    score = qr[:, :, idx] + content
    p = np.exp(score - score.max(axis=-1, keepdims=True))
    p = p / p.sum(axis=-1, keepdims=True)
    y = np.einsum('htn,nhd->thd', p, v)
    k2 = ln(y @ f64(Wk2) + f64(bk2)[:, 0], gain_k2, shift_k2)
    v2 = ln(y @ f64(Wv2) + f64(bv2)[:, 0], gain_v2, shift_v2)
    keys = np.concatenate([k2.reshape(T, E), k.reshape(N, E)], axis=0)
    vals = np.concatenate([v2.reshape(T, E), v.reshape(N, E)], axis=0)
    return np.concatenate([keys, vals], axis=1)

@@ -1,0 +1,264 @@
+import concourse.mybir as mybir
+from concourse.masks import make_identity
+
+F32 = mybir.dt.float32
+BF16 = mybir.dt.bfloat16
+U16 = mybir.dt.uint16
+ALU = mybir.AluOpType
+FUNC = mybir.ActivationFunctionType
+AXIS = mybir.AxisListType
+
+P = 128
+E = 1024
+D = 64
+T = 64
+S = 2048
+N = 1024
+BANK = 512
+BLOCKS = E // P
+HALVES = E // BANK
+GROUPS = BANK // D
+PER_HALF = BANK // P
+EPS = 1e-5
+
+FLOPS = 2 * (2 * N * E * E + P * E * S + E * T * S + 2 * E * T * N + 2 * T * E * D)
+
+
+def tile_sumthenreg2rpeselfattention_b_kernel(
+    tc, reg_x, sum_x, rel_emb, Wr0, Wk, bk, Wv, bv, gain_k, shift_k, gain_v, shift_v,
+    Wk2, bk2, Wv2, bv2, gain_k2, shift_k2, gain_v2, shift_v2, offs, out,
+):
+    nc = tc.nc
+
+    def row_on_all_partitions(column):
+        return column.rearrange("n o -> (n o)").partition_broadcast(P)
+
+    with (
+        tc.tile_pool(name="held", bufs=1) as held,
+        tc.psum_pool(name="banks", bufs=8) as banks,
+    ):
+        offsets = held.tile([P, N // 16], U16, name="offsets")
+        nc.sync.dma_start(offsets[:], offs)
+
+        x_sb = held.tile([P, BLOCKS, N], BF16, name="x_sb")
+        wk_sb = held.tile([P, BLOCKS, E], BF16, name="wk_sb")
+        wv_sb = held.tile([P, BLOCKS, E], BF16, name="wv_sb")
+        q_bd = held.tile([P, BLOCKS, P], BF16, name="q_bd")
+        qr = [held.tile([P, S], F32, name=f"qr{b}") for b in range(BLOCKS)]
+
+        with (
+            tc.tile_pool(name="early", bufs=1) as early,
+            tc.tile_pool(name="stage", bufs=2) as stage,
+        ):
+            sum_sb = early.tile([P, BLOCKS, T], BF16, name="sum_sb")
+            nc.sync.dma_start(sum_sb[:], sum_x.rearrange("(b p) t -> p b t", p=P))
+            wr0_sb = early.tile([P, E], BF16, name="wr0_sb")
+            nc.sync.dma_start(wr0_sb[:], Wr0)
+            rel_bf = early.tile([P, S], BF16, name="rel_bf")
+            for n in range(S // BANK):
+                rel_f = stage.tile([P, BANK], F32, name="rel_f")
+                nc.sync.dma_start(rel_f[:], rel_emb[:, n * BANK : (n + 1) * BANK])
+                nc.vector.tensor_copy(rel_bf[:, n * BANK : (n + 1) * BANK], rel_f[:])
+
+            x_blocks = reg_x.rearrange("(c p) j -> c p j", p=P)
+            wk_blocks = Wk.rearrange("(c p) e -> c p e", p=P)
+            wv_blocks = Wv.rearrange("(c p) e -> c p e", p=P)
+            for c in range(BLOCKS):
+                nc.sync.dma_start(x_sb[:, c, :], x_blocks[c])
+                nc.sync.dma_start(wk_sb[:, c, :], wk_blocks[c])
+
+            nc.vector.memset(q_bd[:], 0.0)
+            nc.vector.tensor_scalar_mul(q_bd[0:D, :, 0:T], sum_sb[0:D, :, :], 0.125)
+            nc.vector.tensor_scalar_mul(q_bd[D:P, :, T:P], sum_sb[D:P, :, :], 0.125)
+
+            for b in range(BLOCKS):
+                r0_bf = stage.tile([P, S], BF16, name="r0_bf")
+                for m in range(S // (2 * BANK)):
+                    r0_ps = banks.tile([P, 2 * BANK], BF16, name="r0_ps", tag="bank")
+                    for n in range(2):
+                        col = (2 * m + n) * BANK
+                        nc.tensor.matmul(
+                            r0_ps[:, n * BANK : (n + 1) * BANK],
+                            lhsT=wr0_sb[:, b * P : (b + 1) * P],
+                            rhs=rel_bf[:, col : col + BANK],
+                            start=True, stop=True,
+                        )
+                    nc.vector.tensor_copy(r0_bf[:, 2 * m * BANK : 2 * (m + 1) * BANK], r0_ps[:])
+                for n in range(S // BANK):
+                    qr_ps = banks.tile([P, BANK], F32, name="qr_ps", tag="bank")
+                    nc.tensor.matmul(
+                        qr_ps[:], lhsT=q_bd[:, b, :], rhs=r0_bf[:, n * BANK : (n + 1) * BANK],
+                        start=True, stop=True,
+                    )
+                    nc.scalar.copy(qr[b][:, n * BANK : (n + 1) * BANK], qr_ps[:])
+
+        bias_k = held.tile([P, E], F32, name="bias_k")
+        nc.sync.dma_start(bias_k[:], row_on_all_partitions(bk))
+        rows = {}
+        for name, column in (("gain_k", gain_k), ("shift_k", shift_k), ("gain_v", gain_v), ("shift_v", shift_v)):
+            rows[name] = held.tile([P, D], F32, name=name)
+            nc.sync.dma_start(rows[name][:], row_on_all_partitions(column))
+        for c in range(BLOCKS):
+            nc.sync.dma_start(wv_sb[:, c, :], wv_blocks[c])
+        bias_v = held.tile([P, E], F32, name="bias_v")
+        nc.sync.dma_start(bias_v[:], row_on_all_partitions(bv))
+        for name, left, right in (("bias_2", bk2, bv2), ("gain_2", gain_k2, gain_v2), ("shift_2", shift_k2, shift_v2)):
+            rows[name] = held.tile([P, 2 * D], F32, name=name)
+            nc.sync.dma_start(rows[name][:, 0:D], row_on_all_partitions(left))
+            nc.sync.dma_start(rows[name][:, D : 2 * D], row_on_all_partitions(right))
+        w2_sb = held.tile([P, 2 * D], BF16, name="w2_sb")
+        for first in (0, D):
+            nc.sync.dma_start(w2_sb[first : first + D, 0:D], Wk2)
+            nc.sync.dma_start(w2_sb[first : first + D, D : 2 * D], Wv2)
+
+        ident_f = held.tile([P, P], F32, name="ident_f")
+        make_identity(nc, ident_f[:])
+        ident_b = held.tile([P, P], BF16, name="ident_b")
+        make_identity(nc, ident_b[:])
+        minus_half = held.tile([P, GROUPS], F32, name="minus_half")
+        nc.vector.memset(minus_half[:], -0.5)
+
+        k_t = held.tile([P, BLOCKS, N], BF16, name="k_t")
+        v_bf = held.tile([P, BLOCKS, E], BF16, name="v_bf")
+        p_t = [held.tile([P, BLOCKS, P], BF16, name=f"p_t{b}") for b in range(BLOCKS)]
+        y_bd = held.tile([P, BLOCKS, P], BF16, name="y_bd")
+        nc.vector.memset(y_bd[:], 0.0)
+        sum_exp = held.tile([P, BLOCKS], F32, name="sum_exp")
+        inv_sum = held.tile([P, BLOCKS], F32, name="inv_sum")
+        z = held.tile([P, HALVES, BANK], F32, name="z")
+
+        with (
+            tc.tile_pool(name="work", bufs=3) as work,
+            tc.tile_pool(name="small", bufs=4) as small,
+            tc.tile_pool(name="att", bufs=2) as att,
+        ):
+
+            def layer_norm(u, gain, shift):
+                stats = small.tile([P, GROUPS, 6], F32, name="stats")
+                mean_var = small.tile([P, GROUPS, 2], F32, name="mean_var")
+                for g in range(GROUPS):
+                    nc.vector.bn_stats(stats[:, g, :], u[:, g * D : (g + 1) * D])
+                    nc.vector.bn_aggr(mean_var[:, g, :], stats[:, g, :])
+                var_eps = small.tile([P, GROUPS], F32, name="var_eps")
+                nc.vector.tensor_scalar_add(var_eps[:], mean_var[:, :, 1], EPS)
+                rstd = small.tile([P, GROUPS], F32, name="rstd")
+                nc.gpsimd.tensor_tensor(rstd[:], var_eps[:], minus_half[:], ALU.pow)
+                shift_mean = small.tile([P, GROUPS], F32, name="shift_mean")
+                nc.vector.scalar_tensor_tensor(shift_mean[:], mean_var[:, :, 0], -1.0, rstd[:], ALU.mult, ALU.mult)
+                centred = work.tile([P, BANK], F32, name="centred")
+                for g in range(GROUPS):
+                    nc.scalar.activation(
+                        centred[:, g * D : (g + 1) * D], u[:, g * D : (g + 1) * D], FUNC.Identity,
+                        bias=shift_mean[:, g : g + 1], scale=rstd[:, g : g + 1],
+                    )
+                period = gain.shape[1]
+                shape = [P, BANK // period, period]
+                by_period = centred[:].rearrange("p (r c) -> p r c", c=period)
+                nc.gpsimd.tensor_tensor(by_period, by_period, gain[:].unsqueeze(1).to_broadcast(shape), ALU.mult)
+                normed = work.tile([P, BANK], F32, name="normed")
+                nc.gpsimd.tensor_tensor(
+                    normed[:].rearrange("p (r c) -> p r c", c=period), by_period,
+                    shift[:].unsqueeze(1).to_broadcast(shape), ALU.add,
+                )
+                return normed
+
+            def project(w_sb, bias, gain, shift, half, jb, first_col):
+                cols = slice(half * BANK, (half + 1) * BANK)
+                acc = banks.tile([P, BANK], F32, name="acc", tag="bank")
+                for c in range(BLOCKS):
+                    nc.tensor.matmul(
+                        acc[:], lhsT=x_sb[:, c, jb * P : (jb + 1) * P], rhs=w_sb[:, c, cols],
+                        start=(c == 0), stop=(c == BLOCKS - 1),
+                    )
+                u = work.tile([P, BANK], F32, name="u")
+                nc.vector.tensor_tensor(u[:], acc[:], bias[:, cols], ALU.add)
+                normed = layer_norm(u, gain, shift)
+                nc.sync.dma_start(
+                    out[T + jb * P : T + (jb + 1) * P, first_col + half * BANK : first_col + (half + 1) * BANK],
+                    normed[:],
+                )
+                return normed
+
+            def make_k(half, jb):
+                k_tile = project(wk_sb, bias_k, rows["gain_k"], rows["shift_k"], half, jb, 0)
+                flipped = banks.tile([P, PER_HALF, P], F32, name="flipped", tag="bank")
+                for i in range(PER_HALF):
+                    nc.tensor.transpose(flipped[:, i, :], k_tile[:, i * P : (i + 1) * P], ident_f[:])
+                nc.scalar.copy(k_t[:, half * PER_HALF : (half + 1) * PER_HALF, jb * P : (jb + 1) * P], flipped[:])
+
+            def make_v(half, jb):
+                v_tile = project(wv_sb, bias_v, rows["gain_v"], rows["shift_v"], half, jb, E)
+                nc.scalar.copy(v_bf[:, jb, half * BANK : (half + 1) * BANK], v_tile[:])
+
+            def attend(b):
+                content = att.tile([P, N], F32, name="content")
+                for n in range(N // BANK):
+                    content_ps = banks.tile([P, BANK], F32, name="content_ps", tag="bank")
+                    nc.tensor.matmul(
+                        content_ps[:], lhsT=q_bd[:, b, :], rhs=k_t[:, b, n * BANK : (n + 1) * BANK],
+                        start=True, stop=True,
+                    )
+                    nc.scalar.copy(content[:, n * BANK : (n + 1) * BANK], content_ps[:])
+                score = att.tile([P, N], F32, name="score")
+                nc.vector.tensor_tensor(score[:], qr[b][:].indirect(offsets[:]), content[:], ALU.add)
+                top = small.tile([P, 1], F32, name="top")
+                nc.vector.reduce_max(top[:], score[:], axis=AXIS.X)
+                minus_top = small.tile([P, 1], F32, name="minus_top")
+                nc.vector.tensor_scalar_mul(minus_top[:], top[:], -1.0)
+                p = att.tile([P, N], BF16, name="p")
+                nc.scalar.activation(
+                    p[:], score[:], FUNC.Exp, bias=minus_top[:], scale=1.0, accum_out=sum_exp[:, b : b + 1]
+                )
+                p_t_ps = banks.tile([P, BLOCKS, P], BF16, name="p_t_ps", tag="bank")
+                for jb in range(BLOCKS):
+                    nc.tensor.transpose(p_t_ps[:, jb, :], p[:, jb * P : (jb + 1) * P], ident_b[:])
+                nc.scalar.copy(p_t[b][:], p_t_ps[:])
+
+            def mix(b):
+                y_ps = banks.tile([P, P], F32, name="y_ps", tag="bank")
+                for jb in range(BLOCKS):
+                    nc.tensor.matmul(
+                        y_ps[:], lhsT=v_bf[:, jb, b * P : (b + 1) * P], rhs=p_t[b][:, jb, :],
+                        start=(jb == 0), stop=(jb == BLOCKS - 1),
+                    )
+                nc.vector.tensor_copy(y_bd[0:D, b, 0:T], y_ps[0:D, 0:T])
+                nc.vector.tensor_copy(y_bd[D:P, b, T:P], y_ps[D:P, T:P])
+                z_ps = banks.tile([P, 2 * D], F32, name="z_ps", tag="bank")
+                nc.tensor.matmul(z_ps[:], lhsT=y_bd[:, b, :], rhs=w2_sb[:], start=True, stop=True)
+                nc.vector.reciprocal(inv_sum[:, b : b + 1], sum_exp[:, b : b + 1])
+                i = b % PER_HALF
+                nc.vector.scalar_tensor_tensor(
+                    z[:, b // PER_HALF, i * P : (i + 1) * P], z_ps[:], inv_sum[:, b : b + 1],
+                    rows["bias_2"][:], ALU.mult, ALU.add,
+                )
+
+            summary_rows = out[0:T, :].rearrange("t (s b h a) -> h s t b a", s=2, b=BLOCKS, h=2, a=D)
+
+            def finish(half):
+                normed = layer_norm(z[:, half, :], rows["gain_2"], rows["shift_2"])
+                by_block = normed[:].rearrange("p (b s a) -> p b s a", s=2, a=D)
+                for h in range(2):
+                    for s in range(2):
+                        nc.sync.dma_start(
+                            summary_rows[h, s][:, half * PER_HALF : (half + 1) * PER_HALF, :],
+                            by_block[h * T : (h + 1) * T, :, s, :],
+                        )
+
+            for jb in range(BLOCKS):
+                make_k(0, jb)
+            for jb in range(BLOCKS):
+                make_k(1, jb)
+                if jb % 2 == 1:
+                    attend(jb // 2)
+            for jb in range(BLOCKS):
+                make_v(0, jb)
+                if jb % 2 == 1:
+                    attend(PER_HALF + jb // 2)
+            for jb in range(BLOCKS):
+                make_v(1, jb)
+                if jb % 2 == 1:
+                    mix(jb // 2)
+            finish(0)
+            for b in range(PER_HALF, BLOCKS):
+                mix(b)
+            finish(1)

@@ -20,6 +20,8 @@ HALVES = E // BANK
 GROUPS = BANK // D
 PER_HALF = BANK // P
 EPS = 1e-5
+SPACING = 3
+FLIP_LAG = 4
 
 FLOPS = 2 * (2 * N * E * E + P * E * S + E * T * S + 2 * E * T * N + 2 * T * E * D)
 
@@ -71,26 +73,31 @@ def tile_sumthenreg2rpeselfattention_b_kernel(
             nc.vector.tensor_scalar_mul(q_bd[0:D, :, 0:T], sum_sb[0:D, :, :], 0.125)
             nc.vector.tensor_scalar_mul(q_bd[D:P, :, T:P], sum_sb[D:P, :, :], 0.125)
 
+            ident_b = held.tile([P, P], BF16, name="ident_b")
+            make_identity(nc, ident_b[:])
+            wr0_t_ps = banks.tile([P, BLOCKS, P], BF16, name="wr0_t_ps", tag="bank")
             for b in range(BLOCKS):
-                r0_bf = stage.tile([P, S], BF16, name="r0_bf")
-                for m in range(S // (2 * BANK)):
-                    r0_ps = banks.tile([P, 2 * BANK], BF16, name="r0_ps", tag="bank")
-                    for n in range(2):
-                        col = (2 * m + n) * BANK
-                        nc.tensor.matmul(
-                            r0_ps[:, n * BANK : (n + 1) * BANK],
-                            lhsT=wr0_sb[:, b * P : (b + 1) * P],
-                            rhs=rel_bf[:, col : col + BANK],
-                            start=True, stop=True,
-                        )
-                    nc.vector.tensor_copy(r0_bf[:, 2 * m * BANK : 2 * (m + 1) * BANK], r0_ps[:])
+                nc.tensor.transpose(wr0_t_ps[:, b, :], wr0_sb[:, b * P : (b + 1) * P], ident_b[:])
+            wr0_t = early.tile([P, BLOCKS, P], BF16, name="wr0_t")
+            nc.vector.tensor_copy(wr0_t[:], wr0_t_ps[:])
+            wq_bf = early.tile([P, BLOCKS, P], BF16, name="wq_bf")
+            for half in range(HALVES):
+                wq_ps = banks.tile([P, PER_HALF, P], F32, name="wq_ps", tag="bank")
+                for n in range(PER_HALF):
+                    b = half * PER_HALF + n
+                    nc.tensor.matmul(wq_ps[:, n, :], lhsT=wr0_t[:, b, :], rhs=q_bd[:, b, :], start=True, stop=True)
+                nc.vector.tensor_copy(wq_bf[:, half * PER_HALF : (half + 1) * PER_HALF, :], wq_ps[:])
+            for b in range(BLOCKS):
                 for n in range(S // BANK):
                     qr_ps = banks.tile([P, BANK], F32, name="qr_ps", tag="bank")
                     nc.tensor.matmul(
-                        qr_ps[:], lhsT=q_bd[:, b, :], rhs=r0_bf[:, n * BANK : (n + 1) * BANK],
+                        qr_ps[:], lhsT=wq_bf[:, b, :], rhs=rel_bf[:, n * BANK : (n + 1) * BANK],
                         start=True, stop=True,
                     )
-                    nc.scalar.copy(qr[b][:, n * BANK : (n + 1) * BANK], qr_ps[:])
+                    if n % 2 == 0:
+                        nc.scalar.copy(qr[b][:, n * BANK : (n + 1) * BANK], qr_ps[:])
+                    else:
+                        nc.vector.tensor_copy(qr[b][:, n * BANK : (n + 1) * BANK], qr_ps[:])
 
         bias_k = held.tile([P, E], F32, name="bias_k")
         nc.sync.dma_start(bias_k[:], row_on_all_partitions(bk))
@@ -113,10 +120,6 @@ def tile_sumthenreg2rpeselfattention_b_kernel(
 
         ident_f = held.tile([P, P], F32, name="ident_f")
         make_identity(nc, ident_f[:])
-        ident_b = held.tile([P, P], BF16, name="ident_b")
-        make_identity(nc, ident_b[:])
-        minus_half = held.tile([P, GROUPS], F32, name="minus_half")
-        nc.vector.memset(minus_half[:], -0.5)
 
         k_t = held.tile([P, BLOCKS, N], BF16, name="k_t")
         v_bf = held.tile([P, BLOCKS, E], BF16, name="v_bf")
@@ -127,22 +130,31 @@ def tile_sumthenreg2rpeselfattention_b_kernel(
         inv_sum = held.tile([P, BLOCKS], F32, name="inv_sum")
         z = held.tile([P, HALVES, BANK], F32, name="z")
 
+        gain_col = held.tile([P, 1], F32, name="gain_col")
+        shift_col = held.tile([P, 1], F32, name="shift_col")
+        for first in (0, D):
+            nc.sync.dma_start(gain_col[first : first + D, :], gain_k)
+            nc.sync.dma_start(shift_col[first : first + D, :], shift_k)
+
         with (
             tc.tile_pool(name="work", bufs=3) as work,
             tc.tile_pool(name="small", bufs=4) as small,
             tc.tile_pool(name="att", bufs=2) as att,
         ):
-
-            def layer_norm(u, gain, shift):
+            def ln_stats(u):
                 stats = small.tile([P, GROUPS, 6], F32, name="stats")
                 mean_var = small.tile([P, GROUPS, 2], F32, name="mean_var")
                 for g in range(GROUPS):
                     nc.vector.bn_stats(stats[:, g, :], u[:, g * D : (g + 1) * D])
+                for g in range(GROUPS):
                     nc.vector.bn_aggr(mean_var[:, g, :], stats[:, g, :])
                 var_eps = small.tile([P, GROUPS], F32, name="var_eps")
                 nc.vector.tensor_scalar_add(var_eps[:], mean_var[:, :, 1], EPS)
                 rstd = small.tile([P, GROUPS], F32, name="rstd")
-                nc.gpsimd.tensor_tensor(rstd[:], var_eps[:], minus_half[:], ALU.pow)
+                nc.scalar.activation(rstd[:], var_eps[:], FUNC.Abs_reciprocal_sqrt)
+                return mean_var, rstd
+
+            def ln_centre(u, mean_var, rstd):
                 shift_mean = small.tile([P, GROUPS], F32, name="shift_mean")
                 nc.vector.scalar_tensor_tensor(shift_mean[:], mean_var[:, :, 0], -1.0, rstd[:], ALU.mult, ALU.mult)
                 centred = work.tile([P, BANK], F32, name="centred")
@@ -151,46 +163,69 @@ def tile_sumthenreg2rpeselfattention_b_kernel(
                         centred[:, g * D : (g + 1) * D], u[:, g * D : (g + 1) * D], FUNC.Identity,
                         bias=shift_mean[:, g : g + 1], scale=rstd[:, g : g + 1],
                     )
+                return centred
+
+            def ln_affine(centred, gain, shift, gain_engine, shift_engine):
                 period = gain.shape[1]
                 shape = [P, BANK // period, period]
                 by_period = centred[:].rearrange("p (r c) -> p r c", c=period)
-                nc.gpsimd.tensor_tensor(by_period, by_period, gain[:].unsqueeze(1).to_broadcast(shape), ALU.mult)
+                gain_engine.tensor_tensor(by_period, by_period, gain[:].unsqueeze(1).to_broadcast(shape), ALU.mult)
                 normed = work.tile([P, BANK], F32, name="normed")
-                nc.gpsimd.tensor_tensor(
+                shift_engine.tensor_tensor(
                     normed[:].rearrange("p (r c) -> p r c", c=period), by_period,
                     shift[:].unsqueeze(1).to_broadcast(shape), ALU.add,
                 )
                 return normed
 
-            def project(w_sb, bias, gain, shift, half, jb, first_col):
+            tiles = [(kind, half, jb) for kind in ("k", "v") for half in range(HALVES) for jb in range(BLOCKS)]
+            weights = {"k": wk_sb, "v": wv_sb}
+            biases = {"k": bias_k, "v": bias_v}
+            in_flight = {}
+
+            def tile_project(i):
+                kind, half, jb = tiles[i]
                 cols = slice(half * BANK, (half + 1) * BANK)
                 acc = banks.tile([P, BANK], F32, name="acc", tag="bank")
                 for c in range(BLOCKS):
                     nc.tensor.matmul(
-                        acc[:], lhsT=x_sb[:, c, jb * P : (jb + 1) * P], rhs=w_sb[:, c, cols],
+                        acc[:], lhsT=x_sb[:, c, jb * P : (jb + 1) * P], rhs=weights[kind][:, c, cols],
                         start=(c == 0), stop=(c == BLOCKS - 1),
                     )
                 u = work.tile([P, BANK], F32, name="u")
-                nc.vector.tensor_tensor(u[:], acc[:], bias[:, cols], ALU.add)
-                normed = layer_norm(u, gain, shift)
+                nc.vector.tensor_tensor(u[:], acc[:], biases[kind][:, cols], ALU.add)
+                in_flight[i] = (u, ln_stats(u))
+
+            def tile_centre(i):
+                u, (mean_var, rstd) = in_flight[i]
+                in_flight[i] = ln_centre(u, mean_var, rstd)
+
+            def tile_finish(i):
+                kind, half, jb = tiles[i]
+                centred = in_flight[i]
+                if kind == "k":
+                    flipped = banks.tile([P, PER_HALF, P], F32, name="flipped", tag="bank")
+                    for n in range(PER_HALF):
+                        nc.tensor.transpose(flipped[:, n, :], centred[:, n * P : (n + 1) * P], ident_f[:])
+                    nc.scalar.activation(
+                        k_t[:, half * PER_HALF : (half + 1) * PER_HALF, jb * P : (jb + 1) * P], flipped[:],
+                        FUNC.Identity, bias=shift_col[:], scale=gain_col[:],
+                    )
+                normed = ln_affine(centred, rows["gain_" + kind], rows["shift_" + kind], nc.vector, nc.gpsimd)
+                first_col = E if kind == "v" else 0
                 nc.sync.dma_start(
                     out[T + jb * P : T + (jb + 1) * P, first_col + half * BANK : first_col + (half + 1) * BANK],
                     normed[:],
                 )
-                return normed
+                in_flight[i] = normed
 
-            def make_k(half, jb):
-                k_tile = project(wk_sb, bias_k, rows["gain_k"], rows["shift_k"], half, jb, 0)
-                flipped = banks.tile([P, PER_HALF, P], F32, name="flipped", tag="bank")
-                for i in range(PER_HALF):
-                    nc.tensor.transpose(flipped[:, i, :], k_tile[:, i * P : (i + 1) * P], ident_f[:])
-                nc.scalar.copy(k_t[:, half * PER_HALF : (half + 1) * PER_HALF, jb * P : (jb + 1) * P], flipped[:])
+            def tile_round_v(i):
+                kind, half, jb = tiles[i]
+                if kind == "v":
+                    nc.scalar.copy(v_bf[:, jb, half * BANK : (half + 1) * BANK], in_flight[i][:])
 
-            def make_v(half, jb):
-                v_tile = project(wv_sb, bias_v, rows["gain_v"], rows["shift_v"], half, jb, E)
-                nc.scalar.copy(v_bf[:, jb, half * BANK : (half + 1) * BANK], v_tile[:])
+            scores = {}
 
-            def attend(b):
+            def attend_content(b):
                 content = att.tile([P, N], F32, name="content")
                 for n in range(N // BANK):
                     content_ps = banks.tile([P, BANK], F32, name="content_ps", tag="bank")
@@ -199,22 +234,37 @@ def tile_sumthenreg2rpeselfattention_b_kernel(
                         start=True, stop=True,
                     )
                     nc.scalar.copy(content[:, n * BANK : (n + 1) * BANK], content_ps[:])
+                scores[b] = content
+
+            def attend_lookup(b):
                 score = att.tile([P, N], F32, name="score")
-                nc.vector.tensor_tensor(score[:], qr[b][:].indirect(offsets[:]), content[:], ALU.add)
+                nc.vector.tensor_tensor(score[:], qr[b][:].indirect(offsets[:]), scores[b][:], ALU.add)
                 top = small.tile([P, 1], F32, name="top")
                 nc.vector.reduce_max(top[:], score[:], axis=AXIS.X)
                 minus_top = small.tile([P, 1], F32, name="minus_top")
                 nc.vector.tensor_scalar_mul(minus_top[:], top[:], -1.0)
+                scores[b] = (score, minus_top)
+
+            def attend_exp(b):
+                score, minus_top = scores[b]
                 p = att.tile([P, N], BF16, name="p")
                 nc.scalar.activation(
                     p[:], score[:], FUNC.Exp, bias=minus_top[:], scale=1.0, accum_out=sum_exp[:, b : b + 1]
                 )
+                scores[b] = p
+
+            def attend_flip(b):
                 p_t_ps = banks.tile([P, BLOCKS, P], BF16, name="p_t_ps", tag="bank")
                 for jb in range(BLOCKS):
-                    nc.tensor.transpose(p_t_ps[:, jb, :], p[:, jb * P : (jb + 1) * P], ident_b[:])
+                    nc.tensor.transpose(p_t_ps[:, jb, :], scores[b][:, jb * P : (jb + 1) * P], ident_b[:])
                 nc.scalar.copy(p_t[b][:], p_t_ps[:])
 
-            def mix(b):
+            def attend(step, r):
+                b, rest = divmod(r, SPACING)
+                if rest == 0 and 0 <= b < BLOCKS:
+                    step(b)
+
+            def mix_values(b):
                 y_ps = banks.tile([P, P], F32, name="y_ps", tag="bank")
                 for jb in range(BLOCKS):
                     nc.tensor.matmul(
@@ -223,19 +273,20 @@ def tile_sumthenreg2rpeselfattention_b_kernel(
                     )
                 nc.vector.tensor_copy(y_bd[0:D, b, 0:T], y_ps[0:D, 0:T])
                 nc.vector.tensor_copy(y_bd[D:P, b, T:P], y_ps[D:P, T:P])
+                nc.vector.reciprocal(inv_sum[:, b : b + 1], sum_exp[:, b : b + 1])
+
+            def mix_project(b):
                 z_ps = banks.tile([P, 2 * D], F32, name="z_ps", tag="bank")
                 nc.tensor.matmul(z_ps[:], lhsT=y_bd[:, b, :], rhs=w2_sb[:], start=True, stop=True)
-                nc.vector.reciprocal(inv_sum[:, b : b + 1], sum_exp[:, b : b + 1])
-                i = b % PER_HALF
+                n = b % PER_HALF
                 nc.vector.scalar_tensor_tensor(
-                    z[:, b // PER_HALF, i * P : (i + 1) * P], z_ps[:], inv_sum[:, b : b + 1],
+                    z[:, b // PER_HALF, n * P : (n + 1) * P], z_ps[:], inv_sum[:, b : b + 1],
                     rows["bias_2"][:], ALU.mult, ALU.add,
                 )
 
             summary_rows = out[0:T, :].rearrange("t (s b h a) -> h s t b a", s=2, b=BLOCKS, h=2, a=D)
 
-            def finish(half):
-                normed = layer_norm(z[:, half, :], rows["gain_2"], rows["shift_2"])
+            def store_summary(half, normed):
                 by_block = normed[:].rearrange("p (b s a) -> p b s a", s=2, a=D)
                 for h in range(2):
                     for s in range(2):
@@ -244,21 +295,37 @@ def tile_sumthenreg2rpeselfattention_b_kernel(
                             by_block[h * T : (h + 1) * T, :, s, :],
                         )
 
-            for jb in range(BLOCKS):
-                make_k(0, jb)
-            for jb in range(BLOCKS):
-                make_k(1, jb)
-                if jb % 2 == 1:
-                    attend(jb // 2)
-            for jb in range(BLOCKS):
-                make_v(0, jb)
-                if jb % 2 == 1:
-                    attend(PER_HALF + jb // 2)
-            for jb in range(BLOCKS):
-                make_v(1, jb)
-                if jb % 2 == 1:
-                    mix(jb // 2)
-            finish(0)
+            n_tiles = len(tiles)
+            half_tiles = BLOCKS
+            first_attend = half_tiles + 2
+            first_mix = 3 * half_tiles + 3
+            for r in range(max(n_tiles + 4, first_attend + SPACING * (BLOCKS - 1) + FLIP_LAG + 1)):
+                if r < n_tiles:
+                    tile_project(r)
+                attend(attend_lookup, r - first_attend - 1)
+                if 0 <= r - 1 < n_tiles:
+                    tile_centre(r - 1)
+                attend(attend_exp, r - first_attend - 2)
+                if 0 <= r - 2 < n_tiles:
+                    tile_finish(r - 2)
+                if 0 <= r - 3 < n_tiles:
+                    tile_round_v(r - 3)
+                attend(attend_content, r - first_attend)
+                attend(attend_flip, r - first_attend - FLIP_LAG)
+                if 0 <= r - first_mix < PER_HALF:
+                    mix_values(r - first_mix)
+                if 0 <= r - first_mix - 1 < PER_HALF:
+                    mix_project(r - first_mix - 1)
+                if r == first_mix + PER_HALF + 1:
+                    z_stats = ln_stats(z[:, 0, :])
+                if r == first_mix + PER_HALF + 2:
+                    z_centred = ln_centre(z[:, 0, :], z_stats[0], z_stats[1])
+                if r == first_mix + PER_HALF + 3:
+                    store_summary(0, ln_affine(z_centred, rows["gain_2"], rows["shift_2"], nc.vector, nc.vector))
             for b in range(PER_HALF, BLOCKS):
-                mix(b)
-            finish(1)
+                mix_values(b)
+            for b in range(PER_HALF, BLOCKS):
+                mix_project(b)
+            z_stats = ln_stats(z[:, 1, :])
+            z_centred = ln_centre(z[:, 1, :], z_stats[0], z_stats[1])
+            store_summary(1, ln_affine(z_centred, rows["gain_2"], rows["shift_2"], nc.vector, nc.vector))

@@ -20,8 +20,12 @@ HALVES = E // BANK
 GROUPS = BANK // D
 PER_HALF = BANK // P
 EPS = 1e-5
-SPACING = 3
-FLIP_LAG = 4
+SPACING = 2
+LOOKUP_LAG = 2
+EXP_LAG = 2
+FLIP_LAG = 3
+Q_ROUND = 3
+QR_BUFS = 4
 
 FLOPS = 2 * (2 * N * E * E + P * E * S + E * T * S + 2 * E * T * N + 2 * T * E * D)
 
@@ -37,6 +41,10 @@ def tile_sumthenreg2rpeselfattention_b_kernel(
 
     with (
         tc.tile_pool(name="held", bufs=1) as held,
+        tc.tile_pool(name="windows", bufs=QR_BUFS) as windows,
+        tc.tile_pool(name="work", bufs=3) as work,
+        tc.tile_pool(name="small", bufs=4) as small,
+        tc.tile_pool(name="att", bufs=PER_HALF) as att,
         tc.psum_pool(name="banks", bufs=8) as banks,
     ):
         offsets = held.tile([P, N // 16], U16, name="offsets")
@@ -45,287 +53,292 @@ def tile_sumthenreg2rpeselfattention_b_kernel(
         x_sb = held.tile([P, BLOCKS, N], BF16, name="x_sb")
         wk_sb = held.tile([P, BLOCKS, E], BF16, name="wk_sb")
         wv_sb = held.tile([P, BLOCKS, E], BF16, name="wv_sb")
+        x_view = reg_x.rearrange("(c p) j -> p c j", p=P)
+        wk_view = Wk.rearrange("(c p) e -> p c e", p=P)
+        wv_view = Wv.rearrange("(c p) e -> p c e", p=P)
+        first, second = slice(0, BANK), slice(BANK, 2 * BANK)
+        bias_k = held.tile([P, E], F32, name="bias_k")
+        bias_v = held.tile([P, E], F32, name="bias_v")
+        rows = {}
+
+        nc.sync.dma_start(wk_sb[:, :, first], wk_view[:, :, first])
+        nc.sync.dma_start(x_sb[:, :, first], x_view[:, :, first])
+        nc.sync.dma_start(bias_k[:], row_on_all_partitions(bk))
+        nc.sync.dma_start(x_sb[:, :, second], x_view[:, :, second])
+        for name, column in (("gain_k", gain_k), ("shift_k", shift_k)):
+            rows[name] = held.tile([P, D], F32, name=name)
+            nc.sync.dma_start(rows[name][:], row_on_all_partitions(column))
+        gain_col = held.tile([P, 1], F32, name="gain_col")
+        shift_col = held.tile([P, 1], F32, name="shift_col")
+        for top in (0, D):
+            nc.sync.dma_start(gain_col[top : top + D, :], gain_k)
+            nc.sync.dma_start(shift_col[top : top + D, :], shift_k)
+        sum_sb = held.tile([P, BLOCKS, T], BF16, name="sum_sb")
+        nc.sync.dma_start(sum_sb[:], sum_x.rearrange("(b p) t -> p b t", p=P))
+        wr0_sb = held.tile([P, E], BF16, name="wr0_sb")
+        nc.sync.dma_start(wr0_sb[:], Wr0)
+        rel_f = held.tile([P, S], F32, name="rel_f")
+        nc.sync.dma_start(rel_f[:], rel_emb)
+        nc.sync.dma_start(wk_sb[:, :, second], wk_view[:, :, second])
+        nc.sync.dma_start(wv_sb[:, :, first], wv_view[:, :, first])
+        nc.sync.dma_start(bias_v[:], row_on_all_partitions(bv))
+        for name, column in (("gain_v", gain_v), ("shift_v", shift_v)):
+            rows[name] = held.tile([P, D], F32, name=name)
+            nc.sync.dma_start(rows[name][:], row_on_all_partitions(column))
+        nc.sync.dma_start(wv_sb[:, :, second], wv_view[:, :, second])
+        for name, left, right in (("bias_2", bk2, bv2), ("gain_2", gain_k2, gain_v2), ("shift_2", shift_k2, shift_v2)):
+            rows[name] = held.tile([P, 2 * D], F32, name=name)
+            nc.sync.dma_start(rows[name][:, 0:D], row_on_all_partitions(left))
+            nc.sync.dma_start(rows[name][:, D : 2 * D], row_on_all_partitions(right))
+        w2_sb = held.tile([P, 2 * D], BF16, name="w2_sb")
+        for top in (0, D):
+            nc.sync.dma_start(w2_sb[top : top + D, 0:D], Wk2)
+            nc.sync.dma_start(w2_sb[top : top + D, D : 2 * D], Wv2)
+
+        ident_f = held.tile([P, P], F32, name="ident_f")
+        make_identity(nc, ident_f[:])
+        ident_b = held.tile([P, P], BF16, name="ident_b")
+        make_identity(nc, ident_b[:])
+
         q_bd = held.tile([P, BLOCKS, P], BF16, name="q_bd")
-        qr = [held.tile([P, S], F32, name=f"qr{b}") for b in range(BLOCKS)]
+        wq_bf = held.tile([P, BLOCKS, P], BF16, name="wq_bf")
+        rel_bf = held.tile([P, S], BF16, name="rel_bf")
+        k_t = held.tile([P, BLOCKS, N], BF16, name="k_t")
+        v_bf = held.tile([P, BLOCKS, E], BF16, name="v_bf")
+        p_t = [held.tile([P, BLOCKS, P], BF16, name=f"p_t{b}") for b in range(BLOCKS)]
+        y_bd = held.tile([P, BLOCKS, P], BF16, name="y_bd")
+        sum_exp = held.tile([P, BLOCKS], F32, name="sum_exp")
+        inv_sum = held.tile([P, BLOCKS], F32, name="inv_sum")
+        z = held.tile([P, HALVES, BANK], F32, name="z")
+        nc.vector.memset(q_bd[:], 0.0)
+        nc.vector.memset(y_bd[:], 0.0)
 
-        with (
-            tc.tile_pool(name="early", bufs=1) as early,
-            tc.tile_pool(name="stage", bufs=2) as stage,
-        ):
-            sum_sb = early.tile([P, BLOCKS, T], BF16, name="sum_sb")
-            nc.sync.dma_start(sum_sb[:], sum_x.rearrange("(b p) t -> p b t", p=P))
-            wr0_sb = early.tile([P, E], BF16, name="wr0_sb")
-            nc.sync.dma_start(wr0_sb[:], Wr0)
-            rel_bf = early.tile([P, S], BF16, name="rel_bf")
-            for n in range(S // BANK):
-                rel_f = stage.tile([P, BANK], F32, name="rel_f")
-                nc.sync.dma_start(rel_f[:], rel_emb[:, n * BANK : (n + 1) * BANK])
-                nc.vector.tensor_copy(rel_bf[:, n * BANK : (n + 1) * BANK], rel_f[:])
-
-            x_blocks = reg_x.rearrange("(c p) j -> c p j", p=P)
-            wk_blocks = Wk.rearrange("(c p) e -> c p e", p=P)
-            wv_blocks = Wv.rearrange("(c p) e -> c p e", p=P)
-            for c in range(BLOCKS):
-                nc.sync.dma_start(x_sb[:, c, :], x_blocks[c])
-                nc.sync.dma_start(wk_sb[:, c, :], wk_blocks[c])
-
-            nc.vector.memset(q_bd[:], 0.0)
+        def prepare_q():
             nc.vector.tensor_scalar_mul(q_bd[0:D, :, 0:T], sum_sb[0:D, :, :], 0.125)
             nc.vector.tensor_scalar_mul(q_bd[D:P, :, T:P], sum_sb[D:P, :, :], 0.125)
-
-            ident_b = held.tile([P, P], BF16, name="ident_b")
-            make_identity(nc, ident_b[:])
             wr0_t_ps = banks.tile([P, BLOCKS, P], BF16, name="wr0_t_ps", tag="bank")
             for b in range(BLOCKS):
                 nc.tensor.transpose(wr0_t_ps[:, b, :], wr0_sb[:, b * P : (b + 1) * P], ident_b[:])
-            wr0_t = early.tile([P, BLOCKS, P], BF16, name="wr0_t")
+            wr0_t = held.tile([P, BLOCKS, P], BF16, name="wr0_t")
             nc.vector.tensor_copy(wr0_t[:], wr0_t_ps[:])
-            wq_bf = early.tile([P, BLOCKS, P], BF16, name="wq_bf")
+            return wr0_t
+
+        def multiply_q(wr0_t):
             for half in range(HALVES):
                 wq_ps = banks.tile([P, PER_HALF, P], F32, name="wq_ps", tag="bank")
                 for n in range(PER_HALF):
                     b = half * PER_HALF + n
                     nc.tensor.matmul(wq_ps[:, n, :], lhsT=wr0_t[:, b, :], rhs=q_bd[:, b, :], start=True, stop=True)
                 nc.vector.tensor_copy(wq_bf[:, half * PER_HALF : (half + 1) * PER_HALF, :], wq_ps[:])
-            for b in range(BLOCKS):
-                for n in range(S // BANK):
-                    qr_ps = banks.tile([P, BANK], F32, name="qr_ps", tag="bank")
-                    nc.tensor.matmul(
-                        qr_ps[:], lhsT=wq_bf[:, b, :], rhs=rel_bf[:, n * BANK : (n + 1) * BANK],
-                        start=True, stop=True,
-                    )
-                    if n % 2 == 0:
-                        nc.scalar.copy(qr[b][:, n * BANK : (n + 1) * BANK], qr_ps[:])
-                    else:
-                        nc.vector.tensor_copy(qr[b][:, n * BANK : (n + 1) * BANK], qr_ps[:])
+            nc.vector.tensor_copy(rel_bf[:], rel_f[:])
 
-        bias_k = held.tile([P, E], F32, name="bias_k")
-        nc.sync.dma_start(bias_k[:], row_on_all_partitions(bk))
-        rows = {}
-        for name, column in (("gain_k", gain_k), ("shift_k", shift_k), ("gain_v", gain_v), ("shift_v", shift_v)):
-            rows[name] = held.tile([P, D], F32, name=name)
-            nc.sync.dma_start(rows[name][:], row_on_all_partitions(column))
-        for c in range(BLOCKS):
-            nc.sync.dma_start(wv_sb[:, c, :], wv_blocks[c])
-        bias_v = held.tile([P, E], F32, name="bias_v")
-        nc.sync.dma_start(bias_v[:], row_on_all_partitions(bv))
-        for name, left, right in (("bias_2", bk2, bv2), ("gain_2", gain_k2, gain_v2), ("shift_2", shift_k2, shift_v2)):
-            rows[name] = held.tile([P, 2 * D], F32, name=name)
-            nc.sync.dma_start(rows[name][:, 0:D], row_on_all_partitions(left))
-            nc.sync.dma_start(rows[name][:, D : 2 * D], row_on_all_partitions(right))
-        w2_sb = held.tile([P, 2 * D], BF16, name="w2_sb")
-        for first in (0, D):
-            nc.sync.dma_start(w2_sb[first : first + D, 0:D], Wk2)
-            nc.sync.dma_start(w2_sb[first : first + D, D : 2 * D], Wv2)
+        qr = {}
 
-        ident_f = held.tile([P, P], F32, name="ident_f")
-        make_identity(nc, ident_f[:])
-
-        k_t = held.tile([P, BLOCKS, N], BF16, name="k_t")
-        v_bf = held.tile([P, BLOCKS, E], BF16, name="v_bf")
-        p_t = [held.tile([P, BLOCKS, P], BF16, name=f"p_t{b}") for b in range(BLOCKS)]
-        y_bd = held.tile([P, BLOCKS, P], BF16, name="y_bd")
-        nc.vector.memset(y_bd[:], 0.0)
-        sum_exp = held.tile([P, BLOCKS], F32, name="sum_exp")
-        inv_sum = held.tile([P, BLOCKS], F32, name="inv_sum")
-        z = held.tile([P, HALVES, BANK], F32, name="z")
-
-        gain_col = held.tile([P, 1], F32, name="gain_col")
-        shift_col = held.tile([P, 1], F32, name="shift_col")
-        for first in (0, D):
-            nc.sync.dma_start(gain_col[first : first + D, :], gain_k)
-            nc.sync.dma_start(shift_col[first : first + D, :], shift_k)
-
-        with (
-            tc.tile_pool(name="work", bufs=3) as work,
-            tc.tile_pool(name="small", bufs=4) as small,
-            tc.tile_pool(name="att", bufs=2) as att,
-        ):
-            def ln_stats(u):
-                stats = small.tile([P, GROUPS, 6], F32, name="stats")
-                mean_var = small.tile([P, GROUPS, 2], F32, name="mean_var")
-                for g in range(GROUPS):
-                    nc.vector.bn_stats(stats[:, g, :], u[:, g * D : (g + 1) * D])
-                for g in range(GROUPS):
-                    nc.vector.bn_aggr(mean_var[:, g, :], stats[:, g, :])
-                var_eps = small.tile([P, GROUPS], F32, name="var_eps")
-                nc.vector.tensor_scalar_add(var_eps[:], mean_var[:, :, 1], EPS)
-                rstd = small.tile([P, GROUPS], F32, name="rstd")
-                nc.scalar.activation(rstd[:], var_eps[:], FUNC.Abs_reciprocal_sqrt)
-                return mean_var, rstd
-
-            def ln_centre(u, mean_var, rstd):
-                shift_mean = small.tile([P, GROUPS], F32, name="shift_mean")
-                nc.vector.scalar_tensor_tensor(shift_mean[:], mean_var[:, :, 0], -1.0, rstd[:], ALU.mult, ALU.mult)
-                centred = work.tile([P, BANK], F32, name="centred")
-                for g in range(GROUPS):
-                    nc.scalar.activation(
-                        centred[:, g * D : (g + 1) * D], u[:, g * D : (g + 1) * D], FUNC.Identity,
-                        bias=shift_mean[:, g : g + 1], scale=rstd[:, g : g + 1],
-                    )
-                return centred
-
-            def ln_affine(centred, gain, shift, gain_engine, shift_engine):
-                period = gain.shape[1]
-                shape = [P, BANK // period, period]
-                by_period = centred[:].rearrange("p (r c) -> p r c", c=period)
-                gain_engine.tensor_tensor(by_period, by_period, gain[:].unsqueeze(1).to_broadcast(shape), ALU.mult)
-                normed = work.tile([P, BANK], F32, name="normed")
-                shift_engine.tensor_tensor(
-                    normed[:].rearrange("p (r c) -> p r c", c=period), by_period,
-                    shift[:].unsqueeze(1).to_broadcast(shape), ALU.add,
+        def make_qr(b):
+            qr[b] = windows.tile([P, S], F32, name="qr")
+            for n in range(S // BANK):
+                qr_ps = banks.tile([P, BANK], F32, name="qr_ps", tag="bank")
+                nc.tensor.matmul(
+                    qr_ps[:], lhsT=wq_bf[:, b, :], rhs=rel_bf[:, n * BANK : (n + 1) * BANK], start=True, stop=True
                 )
-                return normed
+                nc.scalar.copy(qr[b][:, n * BANK : (n + 1) * BANK], qr_ps[:])
 
-            tiles = [(kind, half, jb) for kind in ("k", "v") for half in range(HALVES) for jb in range(BLOCKS)]
-            weights = {"k": wk_sb, "v": wv_sb}
-            biases = {"k": bias_k, "v": bias_v}
-            in_flight = {}
+        def ln_stats(u):
+            stats = small.tile([P, GROUPS, 6], F32, name="stats")
+            mean_var = small.tile([P, GROUPS, 2], F32, name="mean_var")
+            for g in range(GROUPS):
+                nc.vector.bn_stats(stats[:, g, :], u[:, g * D : (g + 1) * D])
+            for g in range(GROUPS):
+                nc.vector.bn_aggr(mean_var[:, g, :], stats[:, g, :])
+            var_eps = small.tile([P, GROUPS], F32, name="var_eps")
+            nc.vector.tensor_scalar_add(var_eps[:], mean_var[:, :, 1], EPS)
+            rstd = small.tile([P, GROUPS], F32, name="rstd")
+            nc.scalar.activation(rstd[:], var_eps[:], FUNC.Abs_reciprocal_sqrt)
+            return mean_var, rstd
 
-            def tile_project(i):
-                kind, half, jb = tiles[i]
-                cols = slice(half * BANK, (half + 1) * BANK)
-                acc = banks.tile([P, BANK], F32, name="acc", tag="bank")
-                for c in range(BLOCKS):
-                    nc.tensor.matmul(
-                        acc[:], lhsT=x_sb[:, c, jb * P : (jb + 1) * P], rhs=weights[kind][:, c, cols],
-                        start=(c == 0), stop=(c == BLOCKS - 1),
-                    )
-                u = work.tile([P, BANK], F32, name="u")
-                nc.vector.tensor_tensor(u[:], acc[:], biases[kind][:, cols], ALU.add)
-                in_flight[i] = (u, ln_stats(u))
-
-            def tile_centre(i):
-                u, (mean_var, rstd) = in_flight[i]
-                in_flight[i] = ln_centre(u, mean_var, rstd)
-
-            def tile_finish(i):
-                kind, half, jb = tiles[i]
-                centred = in_flight[i]
-                if kind == "k":
-                    flipped = banks.tile([P, PER_HALF, P], F32, name="flipped", tag="bank")
-                    for n in range(PER_HALF):
-                        nc.tensor.transpose(flipped[:, n, :], centred[:, n * P : (n + 1) * P], ident_f[:])
-                    nc.scalar.activation(
-                        k_t[:, half * PER_HALF : (half + 1) * PER_HALF, jb * P : (jb + 1) * P], flipped[:],
-                        FUNC.Identity, bias=shift_col[:], scale=gain_col[:],
-                    )
-                normed = ln_affine(centred, rows["gain_" + kind], rows["shift_" + kind], nc.vector, nc.gpsimd)
-                first_col = E if kind == "v" else 0
-                nc.sync.dma_start(
-                    out[T + jb * P : T + (jb + 1) * P, first_col + half * BANK : first_col + (half + 1) * BANK],
-                    normed[:],
-                )
-                in_flight[i] = normed
-
-            def tile_round_v(i):
-                kind, half, jb = tiles[i]
-                if kind == "v":
-                    nc.scalar.copy(v_bf[:, jb, half * BANK : (half + 1) * BANK], in_flight[i][:])
-
-            scores = {}
-
-            def attend_content(b):
-                content = att.tile([P, N], F32, name="content")
-                for n in range(N // BANK):
-                    content_ps = banks.tile([P, BANK], F32, name="content_ps", tag="bank")
-                    nc.tensor.matmul(
-                        content_ps[:], lhsT=q_bd[:, b, :], rhs=k_t[:, b, n * BANK : (n + 1) * BANK],
-                        start=True, stop=True,
-                    )
-                    nc.scalar.copy(content[:, n * BANK : (n + 1) * BANK], content_ps[:])
-                scores[b] = content
-
-            def attend_lookup(b):
-                score = att.tile([P, N], F32, name="score")
-                nc.vector.tensor_tensor(score[:], qr[b][:].indirect(offsets[:]), scores[b][:], ALU.add)
-                top = small.tile([P, 1], F32, name="top")
-                nc.vector.reduce_max(top[:], score[:], axis=AXIS.X)
-                minus_top = small.tile([P, 1], F32, name="minus_top")
-                nc.vector.tensor_scalar_mul(minus_top[:], top[:], -1.0)
-                scores[b] = (score, minus_top)
-
-            def attend_exp(b):
-                score, minus_top = scores[b]
-                p = att.tile([P, N], BF16, name="p")
+        def ln_centre(u, mean_var, rstd):
+            shift_mean = small.tile([P, GROUPS], F32, name="shift_mean")
+            nc.vector.scalar_tensor_tensor(shift_mean[:], mean_var[:, :, 0], -1.0, rstd[:], ALU.mult, ALU.mult)
+            centred = work.tile([P, BANK], F32, name="centred")
+            for g in range(GROUPS):
                 nc.scalar.activation(
-                    p[:], score[:], FUNC.Exp, bias=minus_top[:], scale=1.0, accum_out=sum_exp[:, b : b + 1]
+                    centred[:, g * D : (g + 1) * D], u[:, g * D : (g + 1) * D], FUNC.Identity,
+                    bias=shift_mean[:, g : g + 1], scale=rstd[:, g : g + 1],
                 )
-                scores[b] = p
+            return centred
 
-            def attend_flip(b):
-                p_t_ps = banks.tile([P, BLOCKS, P], BF16, name="p_t_ps", tag="bank")
-                for jb in range(BLOCKS):
-                    nc.tensor.transpose(p_t_ps[:, jb, :], scores[b][:, jb * P : (jb + 1) * P], ident_b[:])
-                nc.scalar.copy(p_t[b][:], p_t_ps[:])
+        def ln_affine(centred, gain, shift, gain_engine, shift_engine):
+            period = gain.shape[1]
+            shape = [P, BANK // period, period]
+            by_period = centred[:].rearrange("p (r c) -> p r c", c=period)
+            gain_engine.tensor_tensor(by_period, by_period, gain[:].unsqueeze(1).to_broadcast(shape), ALU.mult)
+            normed = work.tile([P, BANK], F32, name="normed")
+            shift_engine.tensor_tensor(
+                normed[:].rearrange("p (r c) -> p r c", c=period), by_period,
+                shift[:].unsqueeze(1).to_broadcast(shape), ALU.add,
+            )
+            return normed
 
-            def attend(step, r):
-                b, rest = divmod(r, SPACING)
-                if rest == 0 and 0 <= b < BLOCKS:
-                    step(b)
+        tiles = [(kind, half, jb) for kind in ("k", "v") for half in range(HALVES) for jb in range(BLOCKS)]
+        weights = {"k": wk_sb, "v": wv_sb}
+        biases = {"k": bias_k, "v": bias_v}
+        in_flight = {}
 
-            def mix_values(b):
-                y_ps = banks.tile([P, P], F32, name="y_ps", tag="bank")
-                for jb in range(BLOCKS):
+        def tile_project(i):
+            kind, half, jb = tiles[i]
+            cols = slice(half * BANK, (half + 1) * BANK)
+            acc = banks.tile([P, BANK], F32, name="acc", tag="bank")
+            for c in range(BLOCKS):
+                nc.tensor.matmul(
+                    acc[:], lhsT=x_sb[:, c, jb * P : (jb + 1) * P], rhs=weights[kind][:, c, cols],
+                    start=(c == 0), stop=(c == BLOCKS - 1),
+                )
+            u = work.tile([P, BANK], F32, name="u")
+            nc.vector.tensor_tensor(u[:], acc[:], biases[kind][:, cols], ALU.add)
+            in_flight[i] = (u, ln_stats(u))
+
+        def tile_centre(i):
+            u, (mean_var, rstd) = in_flight[i]
+            in_flight[i] = ln_centre(u, mean_var, rstd)
+
+        def tile_finish(i):
+            kind, half, jb = tiles[i]
+            centred = in_flight[i]
+            if kind == "k":
+                flipped = banks.tile([P, PER_HALF, P], F32, name="flipped", tag="bank")
+                for n in range(PER_HALF):
+                    nc.tensor.transpose(flipped[:, n, :], centred[:, n * P : (n + 1) * P], ident_f[:])
+                nc.scalar.activation(
+                    k_t[:, half * PER_HALF : (half + 1) * PER_HALF, jb * P : (jb + 1) * P], flipped[:],
+                    FUNC.Identity, bias=shift_col[:], scale=gain_col[:],
+                )
+            normed = ln_affine(centred, rows["gain_" + kind], rows["shift_" + kind], nc.vector, nc.gpsimd)
+            first_col = E if kind == "v" else 0
+            nc.sync.dma_start(
+                out[T + jb * P : T + (jb + 1) * P, first_col + half * BANK : first_col + (half + 1) * BANK],
+                normed[:],
+            )
+            in_flight[i] = normed
+
+        def tile_round_v(i):
+            kind, half, jb = tiles[i]
+            if kind == "v":
+                nc.scalar.copy(v_bf[:, jb, half * BANK : (half + 1) * BANK], in_flight[i][:])
+
+        scores = {}
+
+        def attend_content(b):
+            content = att.tile([P, N], F32, name="content", bufs=2)
+            for n in range(N // BANK):
+                content_ps = banks.tile([P, BANK], F32, name="content_ps", tag="bank")
+                nc.tensor.matmul(
+                    content_ps[:], lhsT=q_bd[:, b, :], rhs=k_t[:, b, n * BANK : (n + 1) * BANK],
+                    start=True, stop=True,
+                )
+                nc.scalar.copy(content[:, n * BANK : (n + 1) * BANK], content_ps[:])
+            scores[b] = content
+
+        def attend_lookup(b):
+            score = att.tile([P, N], F32, name="score")
+            nc.vector.tensor_tensor(score[:], qr[b][:].indirect(offsets[:]), scores[b][:], ALU.add)
+            top = small.tile([P, 1], F32, name="top")
+            nc.vector.reduce_max(top[:], score[:], axis=AXIS.X)
+            minus_top = small.tile([P, 1], F32, name="minus_top")
+            nc.vector.tensor_scalar_mul(minus_top[:], top[:], -1.0)
+            scores[b] = (score, minus_top)
+
+        def attend_exp(b):
+            score, minus_top = scores[b]
+            p = att.tile([P, N], BF16, name="p")
+            nc.scalar.activation(
+                p[:], score[:], FUNC.Exp, bias=minus_top[:], scale=1.0, accum_out=sum_exp[:, b : b + 1]
+            )
+            scores[b] = p
+
+        def attend_flip(b):
+            p_t_ps = banks.tile([P, BLOCKS, P], BF16, name="p_t_ps", tag="bank")
+            for jb in range(BLOCKS):
+                nc.tensor.transpose(p_t_ps[:, jb, :], scores[b][:, jb * P : (jb + 1) * P], ident_b[:])
+            nc.scalar.copy(p_t[b][:], p_t_ps[:])
+
+        def mix_values(blocks):
+            y_ps = {b: banks.tile([P, P], F32, name="y_ps", tag="bank") for b in blocks}
+            for jb in range(BLOCKS):
+                for b in blocks:
                     nc.tensor.matmul(
-                        y_ps[:], lhsT=v_bf[:, jb, b * P : (b + 1) * P], rhs=p_t[b][:, jb, :],
+                        y_ps[b][:], lhsT=v_bf[:, jb, b * P : (b + 1) * P], rhs=p_t[b][:, jb, :],
                         start=(jb == 0), stop=(jb == BLOCKS - 1),
                     )
-                nc.vector.tensor_copy(y_bd[0:D, b, 0:T], y_ps[0:D, 0:T])
-                nc.vector.tensor_copy(y_bd[D:P, b, T:P], y_ps[D:P, T:P])
+            for b in blocks:
+                nc.vector.tensor_copy(y_bd[0:D, b, 0:T], y_ps[b][0:D, 0:T])
+                nc.vector.tensor_copy(y_bd[D:P, b, T:P], y_ps[b][D:P, T:P])
                 nc.vector.reciprocal(inv_sum[:, b : b + 1], sum_exp[:, b : b + 1])
 
-            def mix_project(b):
-                z_ps = banks.tile([P, 2 * D], F32, name="z_ps", tag="bank")
-                nc.tensor.matmul(z_ps[:], lhsT=y_bd[:, b, :], rhs=w2_sb[:], start=True, stop=True)
-                n = b % PER_HALF
-                nc.vector.scalar_tensor_tensor(
-                    z[:, b // PER_HALF, n * P : (n + 1) * P], z_ps[:], inv_sum[:, b : b + 1],
-                    rows["bias_2"][:], ALU.mult, ALU.add,
-                )
+        def mix_project(b):
+            z_ps = banks.tile([P, 2 * D], F32, name="z_ps", tag="bank")
+            nc.tensor.matmul(z_ps[:], lhsT=y_bd[:, b, :], rhs=w2_sb[:], start=True, stop=True)
+            n = b % PER_HALF
+            nc.vector.scalar_tensor_tensor(
+                z[:, b // PER_HALF, n * P : (n + 1) * P], z_ps[:], inv_sum[:, b : b + 1],
+                rows["bias_2"][:], ALU.mult, ALU.add,
+            )
 
-            summary_rows = out[0:T, :].rearrange("t (s b h a) -> h s t b a", s=2, b=BLOCKS, h=2, a=D)
+        summary_rows = out[0:T, :].rearrange("t (s b h a) -> h s t b a", s=2, b=BLOCKS, h=2, a=D)
 
-            def store_summary(half, normed):
-                by_block = normed[:].rearrange("p (b s a) -> p b s a", s=2, a=D)
-                for h in range(2):
-                    for s in range(2):
-                        nc.sync.dma_start(
-                            summary_rows[h, s][:, half * PER_HALF : (half + 1) * PER_HALF, :],
-                            by_block[h * T : (h + 1) * T, :, s, :],
-                        )
+        def store_summary(half, normed):
+            by_block = normed[:].rearrange("p (b s a) -> p b s a", s=2, a=D)
+            for h in range(2):
+                for s in range(2):
+                    nc.sync.dma_start(
+                        summary_rows[h, s][:, half * PER_HALF : (half + 1) * PER_HALF, :],
+                        by_block[h * T : (h + 1) * T, :, s, :],
+                    )
 
-            n_tiles = len(tiles)
-            half_tiles = BLOCKS
-            first_attend = half_tiles + 2
-            first_mix = 3 * half_tiles + 3
-            for r in range(max(n_tiles + 4, first_attend + SPACING * (BLOCKS - 1) + FLIP_LAG + 1)):
-                if r < n_tiles:
-                    tile_project(r)
-                attend(attend_lookup, r - first_attend - 1)
-                if 0 <= r - 1 < n_tiles:
-                    tile_centre(r - 1)
-                attend(attend_exp, r - first_attend - 2)
-                if 0 <= r - 2 < n_tiles:
-                    tile_finish(r - 2)
-                if 0 <= r - 3 < n_tiles:
-                    tile_round_v(r - 3)
-                attend(attend_content, r - first_attend)
-                attend(attend_flip, r - first_attend - FLIP_LAG)
-                if 0 <= r - first_mix < PER_HALF:
-                    mix_values(r - first_mix)
-                if 0 <= r - first_mix - 1 < PER_HALF:
-                    mix_project(r - first_mix - 1)
-                if r == first_mix + PER_HALF + 1:
-                    z_stats = ln_stats(z[:, 0, :])
-                if r == first_mix + PER_HALF + 2:
-                    z_centred = ln_centre(z[:, 0, :], z_stats[0], z_stats[1])
-                if r == first_mix + PER_HALF + 3:
-                    store_summary(0, ln_affine(z_centred, rows["gain_2"], rows["shift_2"], nc.vector, nc.vector))
-            for b in range(PER_HALF, BLOCKS):
-                mix_values(b)
-            for b in range(PER_HALF, BLOCKS):
-                mix_project(b)
-            z_stats = ln_stats(z[:, 1, :])
-            z_centred = ln_centre(z[:, 1, :], z_stats[0], z_stats[1])
-            store_summary(1, ln_affine(z_centred, rows["gain_2"], rows["shift_2"], nc.vector, nc.vector))
+        def every_block(step, r):
+            b, rest = divmod(r, SPACING)
+            if rest == 0 and 0 <= b < BLOCKS:
+                step(b)
+
+        n_tiles = len(tiles)
+        half_tiles = BLOCKS
+        first_attend = half_tiles + 2
+        first_mix = 3 * half_tiles + 3
+        for r in range(n_tiles + 4):
+            if r < n_tiles:
+                tile_project(r)
+            every_block(attend_lookup, r - first_attend - LOOKUP_LAG)
+            if 0 <= r - 1 < n_tiles:
+                tile_centre(r - 1)
+            for half in range(HALVES):
+                since = r - (first_attend + LOOKUP_LAG + SPACING * (PER_HALF * (half + 1) - 1) + EXP_LAG)
+                if since == 0:
+                    for b in range(half * PER_HALF, (half + 1) * PER_HALF):
+                        attend_exp(b)
+                if 0 <= since - FLIP_LAG < PER_HALF:
+                    attend_flip(half * PER_HALF + since - FLIP_LAG)
+            if 0 <= r - 2 < n_tiles:
+                tile_finish(r - 2)
+            if 0 <= r - 3 < n_tiles:
+                tile_round_v(r - 3)
+            if r == Q_ROUND:
+                wr0_t = prepare_q()
+            if r == Q_ROUND + 1:
+                multiply_q(wr0_t)
+            every_block(make_qr, r - Q_ROUND - 2)
+            every_block(attend_content, r - first_attend)
+            if 0 <= r - first_mix < PER_HALF:
+                mix_values([r - first_mix])
+            if 0 <= r - first_mix - 1 < PER_HALF:
+                mix_project(r - first_mix - 1)
+            if r == first_mix + PER_HALF + 1:
+                z_stats = ln_stats(z[:, 0, :])
+            if r == first_mix + PER_HALF + 2:
+                z_centred = ln_centre(z[:, 0, :], z_stats[0], z_stats[1])
+            if r == first_mix + PER_HALF + 3:
+                store_summary(0, ln_affine(z_centred, rows["gain_2"], rows["shift_2"], nc.vector, nc.vector))
+        mix_values(range(PER_HALF, BLOCKS))
+        for b in range(PER_HALF, BLOCKS):
+            mix_project(b)
+        z_stats = ln_stats(z[:, 1, :])
+        z_centred = ln_centre(z[:, 1, :], z_stats[0], z_stats[1])
+        store_summary(1, ln_affine(z_centred, rows["gain_2"], rows["shift_2"], nc.vector, nc.vector))

@@ -20,6 +20,7 @@ HALVES = E // BANK
 GROUPS = BANK // D
 PER_HALF = BANK // P
 EPS = 1e-5
+
 SPACING = 2
 LOOKUP_LAG = 2
 EXP_LAG = 2
@@ -70,9 +71,9 @@ def tile_sumthenreg2rpeselfattention_b_kernel(
             nc.sync.dma_start(rows[name][:], row_on_all_partitions(column))
         gain_col = held.tile([P, 1], F32, name="gain_col")
         shift_col = held.tile([P, 1], F32, name="shift_col")
-        for top in (0, D):
-            nc.sync.dma_start(gain_col[top : top + D, :], gain_k)
-            nc.sync.dma_start(shift_col[top : top + D, :], shift_k)
+        for head_row in (0, D):
+            nc.sync.dma_start(gain_col[head_row : head_row + D, :], gain_k)
+            nc.sync.dma_start(shift_col[head_row : head_row + D, :], shift_k)
         sum_sb = held.tile([P, BLOCKS, T], BF16, name="sum_sb")
         nc.sync.dma_start(sum_sb[:], sum_x.rearrange("(b p) t -> p b t", p=P))
         wr0_sb = held.tile([P, E], BF16, name="wr0_sb")
@@ -91,9 +92,9 @@ def tile_sumthenreg2rpeselfattention_b_kernel(
             nc.sync.dma_start(rows[name][:, 0:D], row_on_all_partitions(left))
             nc.sync.dma_start(rows[name][:, D : 2 * D], row_on_all_partitions(right))
         w2_sb = held.tile([P, 2 * D], BF16, name="w2_sb")
-        for top in (0, D):
-            nc.sync.dma_start(w2_sb[top : top + D, 0:D], Wk2)
-            nc.sync.dma_start(w2_sb[top : top + D, D : 2 * D], Wv2)
+        for head_row in (0, D):
+            nc.sync.dma_start(w2_sb[head_row : head_row + D, 0:D], Wk2)
+            nc.sync.dma_start(w2_sb[head_row : head_row + D, D : 2 * D], Wv2)
 
         ident_f = held.tile([P, P], F32, name="ident_f")
         make_identity(nc, ident_f[:])
@@ -167,11 +168,11 @@ def tile_sumthenreg2rpeselfattention_b_kernel(
                 )
             return centred
 
-        def ln_affine(centred, gain, shift, gain_engine, shift_engine):
+        def ln_affine(centred, gain, shift, shift_engine):
             period = gain.shape[1]
             shape = [P, BANK // period, period]
             by_period = centred[:].rearrange("p (r c) -> p r c", c=period)
-            gain_engine.tensor_tensor(by_period, by_period, gain[:].unsqueeze(1).to_broadcast(shape), ALU.mult)
+            nc.vector.tensor_tensor(by_period, by_period, gain[:].unsqueeze(1).to_broadcast(shape), ALU.mult)
             normed = work.tile([P, BANK], F32, name="normed")
             shift_engine.tensor_tensor(
                 normed[:].rearrange("p (r c) -> p r c", c=period), by_period,
@@ -212,7 +213,7 @@ def tile_sumthenreg2rpeselfattention_b_kernel(
                     k_t[:, half * PER_HALF : (half + 1) * PER_HALF, jb * P : (jb + 1) * P], flipped[:],
                     FUNC.Identity, bias=shift_col[:], scale=gain_col[:],
                 )
-            normed = ln_affine(centred, rows["gain_" + kind], rows["shift_" + kind], nc.vector, nc.gpsimd)
+            normed = ln_affine(centred, rows["gain_" + kind], rows["shift_" + kind], nc.gpsimd)
             first_col = E if kind == "v" else 0
             nc.sync.dma_start(
                 out[T + jb * P : T + (jb + 1) * P, first_col + half * BANK : first_col + (half + 1) * BANK],
@@ -223,9 +224,9 @@ def tile_sumthenreg2rpeselfattention_b_kernel(
         def tile_round_v(i):
             kind, half, jb = tiles[i]
             if kind == "v":
-                nc.scalar.copy(v_bf[:, jb, half * BANK : (half + 1) * BANK], in_flight[i][:])
+                nc.vector.tensor_copy(v_bf[:, jb, half * BANK : (half + 1) * BANK], in_flight[i][:])
 
-        scores = {}
+        handed_on = {}
 
         def attend_content(b):
             content = att.tile([P, N], F32, name="content", bufs=2)
@@ -236,29 +237,29 @@ def tile_sumthenreg2rpeselfattention_b_kernel(
                     start=True, stop=True,
                 )
                 nc.scalar.copy(content[:, n * BANK : (n + 1) * BANK], content_ps[:])
-            scores[b] = content
+            handed_on[b] = content
 
         def attend_lookup(b):
             score = att.tile([P, N], F32, name="score")
-            nc.vector.tensor_tensor(score[:], qr[b][:].indirect(offsets[:]), scores[b][:], ALU.add)
+            nc.vector.tensor_tensor(score[:], qr[b][:].indirect(offsets[:]), handed_on[b][:], ALU.add)
             top = small.tile([P, 1], F32, name="top")
             nc.vector.reduce_max(top[:], score[:], axis=AXIS.X)
             minus_top = small.tile([P, 1], F32, name="minus_top")
             nc.vector.tensor_scalar_mul(minus_top[:], top[:], -1.0)
-            scores[b] = (score, minus_top)
+            handed_on[b] = (score, minus_top)
 
         def attend_exp(b):
-            score, minus_top = scores[b]
+            score, minus_top = handed_on[b]
             p = att.tile([P, N], BF16, name="p")
             nc.scalar.activation(
                 p[:], score[:], FUNC.Exp, bias=minus_top[:], scale=1.0, accum_out=sum_exp[:, b : b + 1]
             )
-            scores[b] = p
+            handed_on[b] = p
 
         def attend_flip(b):
             p_t_ps = banks.tile([P, BLOCKS, P], BF16, name="p_t_ps", tag="bank")
             for jb in range(BLOCKS):
-                nc.tensor.transpose(p_t_ps[:, jb, :], scores[b][:, jb * P : (jb + 1) * P], ident_b[:])
+                nc.tensor.transpose(p_t_ps[:, jb, :], handed_on[b][:, jb * P : (jb + 1) * P], ident_b[:])
             nc.scalar.copy(p_t[b][:], p_t_ps[:])
 
         def mix_values(blocks):
@@ -303,7 +304,7 @@ def tile_sumthenreg2rpeselfattention_b_kernel(
         half_tiles = BLOCKS
         first_attend = half_tiles + 2
         first_mix = 3 * half_tiles + 3
-        for r in range(n_tiles + 4):
+        for r in range(n_tiles + 3):
             if r < n_tiles:
                 tile_project(r)
             every_block(attend_lookup, r - first_attend - LOOKUP_LAG)
@@ -335,10 +336,10 @@ def tile_sumthenreg2rpeselfattention_b_kernel(
             if r == first_mix + PER_HALF + 2:
                 z_centred = ln_centre(z[:, 0, :], z_stats[0], z_stats[1])
             if r == first_mix + PER_HALF + 3:
-                store_summary(0, ln_affine(z_centred, rows["gain_2"], rows["shift_2"], nc.vector, nc.vector))
+                store_summary(0, ln_affine(z_centred, rows["gain_2"], rows["shift_2"], nc.vector))
         mix_values(range(PER_HALF, BLOCKS))
         for b in range(PER_HALF, BLOCKS):
             mix_project(b)
         z_stats = ln_stats(z[:, 1, :])
         z_centred = ln_centre(z[:, 1, :], z_stats[0], z_stats[1])
-        store_summary(1, ln_affine(z_centred, rows["gain_2"], rows["shift_2"], nc.vector, nc.vector))
+        store_summary(1, ln_affine(z_centred, rows["gain_2"], rows["shift_2"], nc.vector))

@@ -111,6 +111,8 @@ def tile_sumthenreg2rpeselfattention_b_kernel(
         sum_exp = held.tile([P, BLOCKS], F32, name="sum_exp")
         inv_sum = held.tile([P, BLOCKS], F32, name="inv_sum")
         z = held.tile([P, HALVES, BANK], F32, name="z")
+        eps_col = held.tile([P, 1], F32, name="eps_col")
+        nc.vector.memset(eps_col[:], EPS)
         nc.vector.memset(q_bd[:], 0.0)
         nc.vector.memset(y_bd[:], 0.0)
 
@@ -146,20 +148,24 @@ def tile_sumthenreg2rpeselfattention_b_kernel(
 
         def ln_stats(u):
             stats = small.tile([P, GROUPS, 6], F32, name="stats")
-            mean_var = small.tile([P, GROUPS, 2], F32, name="mean_var")
             for g in range(GROUPS):
                 nc.vector.bn_stats(stats[:, g, :], u[:, g * D : (g + 1) * D])
-            for g in range(GROUPS):
-                nc.vector.bn_aggr(mean_var[:, g, :], stats[:, g, :])
-            var_eps = small.tile([P, GROUPS], F32, name="var_eps")
-            nc.vector.tensor_scalar_add(var_eps[:], mean_var[:, :, 1], EPS)
+            mean_2 = small.tile([P, GROUPS], F32, name="mean_2")
+            nc.vector.tensor_tensor(mean_2[:], stats[:, :, 1], stats[:, :, 4], ALU.add)
+            gap = small.tile([P, GROUPS], F32, name="gap")
+            nc.vector.tensor_tensor(gap[:], stats[:, :, 1], stats[:, :, 4], ALU.subtract)
+            var_64 = small.tile([P, GROUPS], F32, name="var_64")
+            nc.vector.tensor_tensor(var_64[:], stats[:, :, 2], stats[:, :, 5], ALU.add)
+            gap_sq = small.tile([P, GROUPS], F32, name="gap_sq")
+            nc.vector.scalar_tensor_tensor(gap_sq[:], gap[:], D / 4.0, gap[:], ALU.mult, ALU.mult)
+            nc.vector.tensor_tensor(var_64[:], var_64[:], gap_sq[:], ALU.add)
             rstd = small.tile([P, GROUPS], F32, name="rstd")
-            nc.scalar.activation(rstd[:], var_eps[:], FUNC.Abs_reciprocal_sqrt)
-            return mean_var, rstd
+            nc.scalar.activation(rstd[:], var_64[:], FUNC.Abs_reciprocal_sqrt, bias=eps_col[:], scale=1.0 / D)
+            return mean_2, rstd
 
-        def ln_centre(u, mean_var, rstd):
+        def ln_centre(u, mean_2, rstd):
             shift_mean = small.tile([P, GROUPS], F32, name="shift_mean")
-            nc.vector.scalar_tensor_tensor(shift_mean[:], mean_var[:, :, 0], -1.0, rstd[:], ALU.mult, ALU.mult)
+            nc.vector.scalar_tensor_tensor(shift_mean[:], mean_2[:], -0.5, rstd[:], ALU.mult, ALU.mult)
             centred = work.tile([P, BANK], F32, name="centred")
             for g in range(GROUPS):
                 nc.scalar.activation(
@@ -199,8 +205,8 @@ def tile_sumthenreg2rpeselfattention_b_kernel(
             in_flight[i] = (u, ln_stats(u))
 
         def tile_centre(i):
-            u, (mean_var, rstd) = in_flight[i]
-            in_flight[i] = ln_centre(u, mean_var, rstd)
+            u, (mean_2, rstd) = in_flight[i]
+            in_flight[i] = ln_centre(u, mean_2, rstd)
 
         def tile_finish(i):
             kind, half, jb = tiles[i]
@@ -224,7 +230,7 @@ def tile_sumthenreg2rpeselfattention_b_kernel(
         def tile_round_v(i):
             kind, half, jb = tiles[i]
             if kind == "v":
-                nc.vector.tensor_copy(v_bf[:, jb, half * BANK : (half + 1) * BANK], in_flight[i][:])
+                nc.scalar.copy(v_bf[:, jb, half * BANK : (half + 1) * BANK], in_flight[i][:])
 
         handed_on = {}
 

import concourse.mybir as mybir
from concourse.masks import make_identity

F32 = mybir.dt.float32
BF16 = mybir.dt.bfloat16
U16 = mybir.dt.uint16
ALU = mybir.AluOpType
FUNC = mybir.ActivationFunctionType
AXIS = mybir.AxisListType

P = 128
E = 1024
D = 64
T = 64
S = 2048
N = 1024
BANK = 512
BLOCKS = E // P
HALVES = E // BANK
GROUPS = BANK // D
PER_HALF = BANK // P
EPS = 1e-5

SPACING = 2
LOOKUP_LAG = 2
EXP_LAG = 2
FLIP_LAG = 3
Q_ROUND = 3
QR_BUFS = 4

FLOPS = 2 * (2 * N * E * E + P * E * S + E * T * S + 2 * E * T * N + 2 * T * E * D)


def tile_sumthenreg2rpeselfattention_b_kernel(
    tc, reg_x, sum_x, rel_emb, Wr0, Wk, bk, Wv, bv, gain_k, shift_k, gain_v, shift_v,
    Wk2, bk2, Wv2, bv2, gain_k2, shift_k2, gain_v2, shift_v2, offs, out,
):
    nc = tc.nc

    def row_on_all_partitions(column):
        return column.rearrange("n o -> (n o)").partition_broadcast(P)

    with (
        tc.tile_pool(name="held", bufs=1) as held,
        tc.tile_pool(name="windows", bufs=QR_BUFS) as windows,
        tc.tile_pool(name="work", bufs=3) as work,
        tc.tile_pool(name="small", bufs=4) as small,
        tc.tile_pool(name="att", bufs=PER_HALF) as att,
        tc.psum_pool(name="banks", bufs=8) as banks,
    ):
        offsets = held.tile([P, N // 16], U16, name="offsets")
        nc.sync.dma_start(offsets[:], offs)

        x_sb = held.tile([P, BLOCKS, N], BF16, name="x_sb")
        wk_sb = held.tile([P, BLOCKS, E], BF16, name="wk_sb")
        wv_sb = held.tile([P, BLOCKS, E], BF16, name="wv_sb")
        x_view = reg_x.rearrange("(c p) j -> p c j", p=P)
        wk_view = Wk.rearrange("(c p) e -> p c e", p=P)
        wv_view = Wv.rearrange("(c p) e -> p c e", p=P)
        first, second = slice(0, BANK), slice(BANK, 2 * BANK)
        bias_k = held.tile([P, E], F32, name="bias_k")
        bias_v = held.tile([P, E], F32, name="bias_v")
        rows = {}

        nc.sync.dma_start(wk_sb[:, :, first], wk_view[:, :, first])
        nc.sync.dma_start(x_sb[:, :, first], x_view[:, :, first])
        nc.sync.dma_start(bias_k[:], row_on_all_partitions(bk))
        nc.sync.dma_start(x_sb[:, :, second], x_view[:, :, second])
        for name, column in (("gain_k", gain_k), ("shift_k", shift_k)):
            rows[name] = held.tile([P, D], F32, name=name)
            nc.sync.dma_start(rows[name][:], row_on_all_partitions(column))
        gain_col = held.tile([P, 1], F32, name="gain_col")
        shift_col = held.tile([P, 1], F32, name="shift_col")
        for head_row in (0, D):
            nc.sync.dma_start(gain_col[head_row : head_row + D, :], gain_k)
            nc.sync.dma_start(shift_col[head_row : head_row + D, :], shift_k)
        sum_sb = held.tile([P, BLOCKS, T], BF16, name="sum_sb")
        nc.sync.dma_start(sum_sb[:], sum_x.rearrange("(b p) t -> p b t", p=P))
        wr0_sb = held.tile([P, E], BF16, name="wr0_sb")
        nc.sync.dma_start(wr0_sb[:], Wr0)
        rel_f = held.tile([P, S], F32, name="rel_f")
        nc.sync.dma_start(rel_f[:], rel_emb)
        nc.sync.dma_start(wk_sb[:, :, second], wk_view[:, :, second])
        nc.sync.dma_start(wv_sb[:, :, first], wv_view[:, :, first])
        nc.sync.dma_start(bias_v[:], row_on_all_partitions(bv))
        for name, column in (("gain_v", gain_v), ("shift_v", shift_v)):
            rows[name] = held.tile([P, D], F32, name=name)
            nc.sync.dma_start(rows[name][:], row_on_all_partitions(column))
        nc.sync.dma_start(wv_sb[:, :, second], wv_view[:, :, second])
        for name, left, right in (("bias_2", bk2, bv2), ("gain_2", gain_k2, gain_v2), ("shift_2", shift_k2, shift_v2)):
            rows[name] = held.tile([P, 2 * D], F32, name=name)
            nc.sync.dma_start(rows[name][:, 0:D], row_on_all_partitions(left))
            nc.sync.dma_start(rows[name][:, D : 2 * D], row_on_all_partitions(right))
        w2_sb = held.tile([P, 2 * D], BF16, name="w2_sb")
        for head_row in (0, D):
            nc.sync.dma_start(w2_sb[head_row : head_row + D, 0:D], Wk2)
            nc.sync.dma_start(w2_sb[head_row : head_row + D, D : 2 * D], Wv2)

        ident_f = held.tile([P, P], F32, name="ident_f")
        make_identity(nc, ident_f[:])
        ident_b = held.tile([P, P], BF16, name="ident_b")
        make_identity(nc, ident_b[:])

        q_bd = held.tile([P, BLOCKS, P], BF16, name="q_bd")
        wq_bf = held.tile([P, BLOCKS, P], BF16, name="wq_bf")
        rel_bf = held.tile([P, S], BF16, name="rel_bf")
        k_t = held.tile([P, BLOCKS, N], BF16, name="k_t")
        v_bf = held.tile([P, BLOCKS, E], BF16, name="v_bf")
        p_t = [held.tile([P, BLOCKS, P], BF16, name=f"p_t{b}") for b in range(BLOCKS)]
        y_bd = held.tile([P, BLOCKS, P], BF16, name="y_bd")
        sum_exp = held.tile([P, BLOCKS], F32, name="sum_exp")
        inv_sum = held.tile([P, BLOCKS], F32, name="inv_sum")
        z = held.tile([P, HALVES, BANK], F32, name="z")
        eps_col = held.tile([P, 1], F32, name="eps_col")
        nc.vector.memset(eps_col[:], EPS)
        nc.vector.memset(q_bd[:], 0.0)
        nc.vector.memset(y_bd[:], 0.0)

        def prepare_q():
            nc.vector.tensor_scalar_mul(q_bd[0:D, :, 0:T], sum_sb[0:D, :, :], 0.125)
            nc.vector.tensor_scalar_mul(q_bd[D:P, :, T:P], sum_sb[D:P, :, :], 0.125)
            wr0_t_ps = banks.tile([P, BLOCKS, P], BF16, name="wr0_t_ps", tag="bank")
            for b in range(BLOCKS):
                nc.tensor.transpose(wr0_t_ps[:, b, :], wr0_sb[:, b * P : (b + 1) * P], ident_b[:])
            wr0_t = held.tile([P, BLOCKS, P], BF16, name="wr0_t")
            nc.vector.tensor_copy(wr0_t[:], wr0_t_ps[:])
            return wr0_t

        def multiply_q(wr0_t):
            for half in range(HALVES):
                wq_ps = banks.tile([P, PER_HALF, P], F32, name="wq_ps", tag="bank")
                for n in range(PER_HALF):
                    b = half * PER_HALF + n
                    nc.tensor.matmul(wq_ps[:, n, :], lhsT=wr0_t[:, b, :], rhs=q_bd[:, b, :], start=True, stop=True)
                nc.vector.tensor_copy(wq_bf[:, half * PER_HALF : (half + 1) * PER_HALF, :], wq_ps[:])
            nc.vector.tensor_copy(rel_bf[:], rel_f[:])

        qr = {}

        def make_qr(b):
            qr[b] = windows.tile([P, S], F32, name="qr")
            for n in range(S // BANK):
                qr_ps = banks.tile([P, BANK], F32, name="qr_ps", tag="bank")
                nc.tensor.matmul(
                    qr_ps[:], lhsT=wq_bf[:, b, :], rhs=rel_bf[:, n * BANK : (n + 1) * BANK], start=True, stop=True
                )
                nc.scalar.copy(qr[b][:, n * BANK : (n + 1) * BANK], qr_ps[:])

        def ln_stats(u):
            stats = small.tile([P, GROUPS, 6], F32, name="stats")
            for g in range(GROUPS):
                nc.vector.bn_stats(stats[:, g, :], u[:, g * D : (g + 1) * D])
            mean_2 = small.tile([P, GROUPS], F32, name="mean_2")
            nc.vector.tensor_tensor(mean_2[:], stats[:, :, 1], stats[:, :, 4], ALU.add)
            gap = small.tile([P, GROUPS], F32, name="gap")
            nc.vector.tensor_tensor(gap[:], stats[:, :, 1], stats[:, :, 4], ALU.subtract)
            var_64 = small.tile([P, GROUPS], F32, name="var_64")
            nc.vector.tensor_tensor(var_64[:], stats[:, :, 2], stats[:, :, 5], ALU.add)
            gap_sq = small.tile([P, GROUPS], F32, name="gap_sq")
            nc.vector.scalar_tensor_tensor(gap_sq[:], gap[:], D / 4.0, gap[:], ALU.mult, ALU.mult)
            nc.vector.tensor_tensor(var_64[:], var_64[:], gap_sq[:], ALU.add)
            rstd = small.tile([P, GROUPS], F32, name="rstd")
            nc.scalar.activation(rstd[:], var_64[:], FUNC.Abs_reciprocal_sqrt, bias=eps_col[:], scale=1.0 / D)
            return mean_2, rstd

        def ln_centre(u, mean_2, rstd):
            shift_mean = small.tile([P, GROUPS], F32, name="shift_mean")
            nc.vector.scalar_tensor_tensor(shift_mean[:], mean_2[:], -0.5, rstd[:], ALU.mult, ALU.mult)
            centred = work.tile([P, BANK], F32, name="centred")
            for g in range(GROUPS):
                nc.scalar.activation(
                    centred[:, g * D : (g + 1) * D], u[:, g * D : (g + 1) * D], FUNC.Identity,
                    bias=shift_mean[:, g : g + 1], scale=rstd[:, g : g + 1],
                )
            return centred

        def ln_affine(centred, gain, shift, shift_engine):
            period = gain.shape[1]
            shape = [P, BANK // period, period]
            by_period = centred[:].rearrange("p (r c) -> p r c", c=period)
            nc.vector.tensor_tensor(by_period, by_period, gain[:].unsqueeze(1).to_broadcast(shape), ALU.mult)
            normed = work.tile([P, BANK], F32, name="normed")
            shift_engine.tensor_tensor(
                normed[:].rearrange("p (r c) -> p r c", c=period), by_period,
                shift[:].unsqueeze(1).to_broadcast(shape), ALU.add,
            )
            return normed

        tiles = [(kind, half, jb) for kind in ("k", "v") for half in range(HALVES) for jb in range(BLOCKS)]
        weights = {"k": wk_sb, "v": wv_sb}
        biases = {"k": bias_k, "v": bias_v}
        in_flight = {}

        def tile_project(i):
            kind, half, jb = tiles[i]
            cols = slice(half * BANK, (half + 1) * BANK)
            acc = banks.tile([P, BANK], F32, name="acc", tag="bank")
            for c in range(BLOCKS):
                nc.tensor.matmul(
                    acc[:], lhsT=x_sb[:, c, jb * P : (jb + 1) * P], rhs=weights[kind][:, c, cols],
                    start=(c == 0), stop=(c == BLOCKS - 1),
                )
            u = work.tile([P, BANK], F32, name="u")
            nc.vector.tensor_tensor(u[:], acc[:], biases[kind][:, cols], ALU.add)
            in_flight[i] = (u, ln_stats(u))

        def tile_centre(i):
            u, (mean_2, rstd) = in_flight[i]
            in_flight[i] = ln_centre(u, mean_2, rstd)

        def tile_finish(i):
            kind, half, jb = tiles[i]
            centred = in_flight[i]
            if kind == "k":
                flipped = banks.tile([P, PER_HALF, P], F32, name="flipped", tag="bank")
                for n in range(PER_HALF):
                    nc.tensor.transpose(flipped[:, n, :], centred[:, n * P : (n + 1) * P], ident_f[:])
                nc.scalar.activation(
                    k_t[:, half * PER_HALF : (half + 1) * PER_HALF, jb * P : (jb + 1) * P], flipped[:],
                    FUNC.Identity, bias=shift_col[:], scale=gain_col[:],
                )
            normed = ln_affine(centred, rows["gain_" + kind], rows["shift_" + kind], nc.gpsimd)
            first_col = E if kind == "v" else 0
            nc.sync.dma_start(
                out[T + jb * P : T + (jb + 1) * P, first_col + half * BANK : first_col + (half + 1) * BANK],
                normed[:],
            )
            in_flight[i] = normed

        def tile_round_v(i):
            kind, half, jb = tiles[i]
            if kind == "v":
                nc.scalar.copy(v_bf[:, jb, half * BANK : (half + 1) * BANK], in_flight[i][:])

        handed_on = {}

        def attend_content(b):
            content = att.tile([P, N], F32, name="content", bufs=2)
            for n in range(N // BANK):
                content_ps = banks.tile([P, BANK], F32, name="content_ps", tag="bank")
                nc.tensor.matmul(
                    content_ps[:], lhsT=q_bd[:, b, :], rhs=k_t[:, b, n * BANK : (n + 1) * BANK],
                    start=True, stop=True,
                )
                nc.scalar.copy(content[:, n * BANK : (n + 1) * BANK], content_ps[:])
            handed_on[b] = content

        def attend_lookup(b):
            score = att.tile([P, N], F32, name="score")
            nc.vector.tensor_tensor(score[:], qr[b][:].indirect(offsets[:]), handed_on[b][:], ALU.add)
            top = small.tile([P, 1], F32, name="top")
            nc.vector.reduce_max(top[:], score[:], axis=AXIS.X)
            minus_top = small.tile([P, 1], F32, name="minus_top")
            nc.vector.tensor_scalar_mul(minus_top[:], top[:], -1.0)
            handed_on[b] = (score, minus_top)

        def attend_exp(b):
            score, minus_top = handed_on[b]
            p = att.tile([P, N], BF16, name="p")
            nc.scalar.activation(
                p[:], score[:], FUNC.Exp, bias=minus_top[:], scale=1.0, accum_out=sum_exp[:, b : b + 1]
            )
            handed_on[b] = p

        def attend_flip(b):
            p_t_ps = banks.tile([P, BLOCKS, P], BF16, name="p_t_ps", tag="bank")
            for jb in range(BLOCKS):
                nc.tensor.transpose(p_t_ps[:, jb, :], handed_on[b][:, jb * P : (jb + 1) * P], ident_b[:])
            nc.scalar.copy(p_t[b][:], p_t_ps[:])

        def mix_values(blocks):
            y_ps = {b: banks.tile([P, P], F32, name="y_ps", tag="bank") for b in blocks}
            for jb in range(BLOCKS):
                for b in blocks:
                    nc.tensor.matmul(
                        y_ps[b][:], lhsT=v_bf[:, jb, b * P : (b + 1) * P], rhs=p_t[b][:, jb, :],
                        start=(jb == 0), stop=(jb == BLOCKS - 1),
                    )
            for b in blocks:
                nc.vector.tensor_copy(y_bd[0:D, b, 0:T], y_ps[b][0:D, 0:T])
                nc.vector.tensor_copy(y_bd[D:P, b, T:P], y_ps[b][D:P, T:P])
                nc.vector.reciprocal(inv_sum[:, b : b + 1], sum_exp[:, b : b + 1])

        def mix_project(b):
            z_ps = banks.tile([P, 2 * D], F32, name="z_ps", tag="bank")
            nc.tensor.matmul(z_ps[:], lhsT=y_bd[:, b, :], rhs=w2_sb[:], start=True, stop=True)
            n = b % PER_HALF
            nc.vector.scalar_tensor_tensor(
                z[:, b // PER_HALF, n * P : (n + 1) * P], z_ps[:], inv_sum[:, b : b + 1],
                rows["bias_2"][:], ALU.mult, ALU.add,
            )

        summary_rows = out[0:T, :].rearrange("t (s b h a) -> h s t b a", s=2, b=BLOCKS, h=2, a=D)

        def store_summary(half, normed):
            by_block = normed[:].rearrange("p (b s a) -> p b s a", s=2, a=D)
            for h in range(2):
                for s in range(2):
                    nc.sync.dma_start(
                        summary_rows[h, s][:, half * PER_HALF : (half + 1) * PER_HALF, :],
                        by_block[h * T : (h + 1) * T, :, s, :],
                    )

        def every_block(step, r):
            b, rest = divmod(r, SPACING)
            if rest == 0 and 0 <= b < BLOCKS:
                step(b)

        n_tiles = len(tiles)
        half_tiles = BLOCKS
        first_attend = half_tiles + 2
        first_mix = 3 * half_tiles + 3
        for r in range(n_tiles + 3):
            if r < n_tiles:
                tile_project(r)
            every_block(attend_lookup, r - first_attend - LOOKUP_LAG)
            if 0 <= r - 1 < n_tiles:
                tile_centre(r - 1)
            for half in range(HALVES):
                since = r - (first_attend + LOOKUP_LAG + SPACING * (PER_HALF * (half + 1) - 1) + EXP_LAG)
                if since == 0:
                    for b in range(half * PER_HALF, (half + 1) * PER_HALF):
                        attend_exp(b)
                if 0 <= since - FLIP_LAG < PER_HALF:
                    attend_flip(half * PER_HALF + since - FLIP_LAG)
            if 0 <= r - 2 < n_tiles:
                tile_finish(r - 2)
            if 0 <= r - 3 < n_tiles:
                tile_round_v(r - 3)
            if r == Q_ROUND:
                wr0_t = prepare_q()
            if r == Q_ROUND + 1:
                multiply_q(wr0_t)
            every_block(make_qr, r - Q_ROUND - 2)
            every_block(attend_content, r - first_attend)
            if 0 <= r - first_mix < PER_HALF:
                mix_values([r - first_mix])
            if 0 <= r - first_mix - 1 < PER_HALF:
                mix_project(r - first_mix - 1)
            if r == first_mix + PER_HALF + 1:
                z_stats = ln_stats(z[:, 0, :])
            if r == first_mix + PER_HALF + 2:
                z_centred = ln_centre(z[:, 0, :], z_stats[0], z_stats[1])
            if r == first_mix + PER_HALF + 3:
                store_summary(0, ln_affine(z_centred, rows["gain_2"], rows["shift_2"], nc.vector))
        mix_values(range(PER_HALF, BLOCKS))
        for b in range(PER_HALF, BLOCKS):
            mix_project(b)
        z_stats = ln_stats(z[:, 1, :])
        z_centred = ln_centre(z[:, 1, :], z_stats[0], z_stats[1])
        store_summary(1, ln_affine(z_centred, rows["gain_2"], rows["shift_2"], nc.vector))
